import numpy as np
import ml_dtypes


def mxq(x, axis, fmt="e4m3"):
    dtype, down = {"e4m3": (ml_dtypes.float8_e4m3fn, 7), "e5m2": (ml_dtypes.float8_e5m2, 14)}[fmt]
    v = np.moveaxis(np.asarray(x, np.float32).astype(ml_dtypes.bfloat16).astype(np.float64), axis, -1)
    blocks = v.reshape(v.shape[:-1] + (-1, 32))
    amax = np.abs(blocks).max(-1, keepdims=True)
    byte = np.maximum(np.where(amax > 0, np.frexp(amax)[1] - 1 + 127, 0) - down, 1)
    scale = np.exp2(byte - 127.0)
    codes = (blocks / scale).astype(np.float32).astype(dtype).astype(np.float64)
    return np.moveaxis((codes * scale).reshape(v.shape), -1, axis)


WIDE = False


def mx_kscale(k):
    if not WIDE:
        return np.ones(k)
    levels = np.array([10, -10, 5, -5, 0])
    a = np.random.permutation(np.resize(levels, k // 512 * 4)).reshape(k // 512, 4)
    idx = np.arange(k)
    return np.exp2(a[idx // 512, idx % 128 // 32])


BF16 = ml_dtypes.bfloat16


def bf(x):
    return np.asarray(x, np.float32).astype(BF16)


def f64(x):
    return np.asarray(x).astype(np.float64)


E2M1 = np.array([0.0, 0.5, 1.0, 1.5, 2.0, 3.0, 4.0, 6.0, -0.0, -0.5, -1.0, -1.5, -2.0, -3.0, -4.0, -6.0])


def pack_weight(w, fmt):
    k, n = w.shape
    w = f64(bf(w)).reshape(k // 32, 32, n)
    amax = np.abs(w).max(1)
    if fmt == "e4m3":
        byte = np.frexp(amax)[1] - 1 + 127 - 7
    else:
        mant, ex = np.frexp(amax / 6.0)
        byte = np.where(mant > 0.5, ex, ex - 1) + 127
    byte = np.clip(np.where(amax > 0, byte, 1), 1, 254)
    scaled = (w * np.exp2(127.0 - byte)[:, None, :]).reshape(k, n).astype(np.float32)
    by_word = np.ascontiguousarray(scaled.reshape(k // 512, 128, 4, n).transpose(0, 1, 3, 2))
    if fmt == "e4m3":
        words = by_word.astype(ml_dtypes.float8_e4m3fn).view(np.uint8)
    else:
        c = by_word.astype(ml_dtypes.float4_e2m1fn).view(np.uint8) & 0xF
        words = c[..., 0::2] | (c[..., 1::2] << 4)
    return np.ascontiguousarray(words), np.ascontiguousarray(byte.astype(np.uint8).reshape(k // 512, 16, n))


def unpack_weight(words, scales, fmt):
    g, p, n, _ = words.shape
    if fmt == "e4m3":
        vals = np.ascontiguousarray(words).view(ml_dtypes.float8_e4m3fn).astype(np.float64)
    else:
        nib = np.empty((g, p, n, 4), np.uint8)
        nib[..., 0::2] = words & 0xF
        nib[..., 1::2] = words >> 4
        vals = E2M1[nib]
    vals = vals * np.repeat(np.exp2(scales.astype(np.float64) - 127.0), 8, axis=1)[..., None]
    return vals.transpose(0, 1, 3, 2).reshape(g * 512, n)

def pack4(w):
    words, scales = pack_weight(w, "e2m1")
    return words.reshape(words.shape[0], 128, -1), scales


def unpack4(words, scales):
    return unpack_weight(words.reshape(words.shape[0], 128, -1, 2), scales, "e2m1")


B, G, DB, DR = 4096, 4, 512, 512


def mish(v):
    return v * np.tanh(np.log(1.0 + np.exp(v)))


def setup_inputs():
    s, t = mx_kscale(DR), mx_kscale(DB)
    BB_feature = bf(np.random.standard_normal((B, G, DB)) * t)
    RF_feature = bf(np.random.standard_normal((B, DR)) * s)
    W_rfrf = np.random.standard_normal((DR, DR)) / np.sqrt(DR) / s
    W_rfrf_words, W_rfrf_scales = pack4(np.ascontiguousarray(W_rfrf.T))
    b_rfrf = bf(np.random.standard_normal(DR) * 0.5)
    W_bbrf = np.random.standard_normal((DR, DB)) * np.sqrt(G / DB) / t
    W_bbrf_words, W_bbrf_scales = pack4(np.ascontiguousarray(W_bbrf.T))
    b_bbrf = bf(np.random.standard_normal(DR) * 0.5)
    return {"BB_feature": BB_feature,
            "RF_feature": RF_feature,
            "W_rfrf_words": W_rfrf_words,
            "W_rfrf_scales": W_rfrf_scales,
            "b_rfrf": b_rfrf,
            "W_bbrf_words": W_bbrf_words,
            "W_bbrf_scales": W_bbrf_scales,
            "b_bbrf": b_bbrf}


def reference(BB_feature, RF_feature, W_rfrf_words, W_rfrf_scales, b_rfrf, W_bbrf_words, W_bbrf_scales, b_bbrf):
    BB_mean = np.mean(f64(BB_feature), axis=-2)
    RF_to_RF = mish((mxq(f64(RF_feature), 1, "e4m3") @ unpack4(W_rfrf_words, W_rfrf_scales)) + f64(b_rfrf))
    BB_to_RF = mish((mxq(BB_mean, 1, "e4m3") @ unpack4(W_bbrf_words, W_bbrf_scales)) + f64(b_bbrf))
    return RF_to_RF + BB_to_RF

@@ -1,0 +1,256 @@
+from contextlib import ExitStack
+
+import concourse.mybir as mybir
+from concourse.masks import make_identity
+
+F32 = mybir.dt.float32
+BF16 = mybir.dt.bfloat16
+I32 = mybir.dt.int32
+U32 = mybir.dt.uint32
+U8 = mybir.dt.uint8
+FP8X4 = mybir.dt.float8_e4m3fn_x4
+FP4X4 = mybir.dt.float4_e2m1fn_x4
+ACT = mybir.ActivationFunctionType
+ALU = mybir.AluOpType
+
+P = 128
+PACK = 4
+TOKENS = 4096
+GROUPS = 4
+WIDTH = 512
+TILES = TOKENS // P
+QUADS = 4
+SAMPLES = P // GROUPS
+BATCH = 8
+BATCHES = TILES // BATCH
+LOAD_AHEAD = 6
+ADD_AHEAD = 4
+TINY = 2.0 ** -60
+
+FLOPS = 2 * 2 * TOKENS * WIDTH * WIDTH
+
+
+def tile_gnn_layer_pa_t_kernel(
+    tc,
+    BB_feature,
+    RF_feature,
+    W_rfrf_words,
+    W_rfrf_scales,
+    b_rfrf,
+    W_bbrf_words,
+    W_bbrf_scales,
+    b_bbrf,
+    out,
+):
+    nc = tc.nc
+    bb_rows = BB_feature.rearrange("b g k -> (b g) k").rearrange(
+        "(i s p) k -> i p s k", s=QUADS, p=P
+    )
+    rf_rows = RF_feature.rearrange("(n s p) k -> n p s k", s=QUADS, p=P)
+
+    def summed_by_adds(i):
+        return i % QUADS == QUADS - 1
+
+    with ExitStack() as stack:
+        consts = stack.enter_context(tc.tile_pool(name="consts", bufs=1))
+        bb_pool = stack.enter_context(tc.tile_pool(name="bb", bufs=LOAD_AHEAD + 2))
+        rf_pool = stack.enter_context(tc.tile_pool(name="rf", bufs=3))
+        pack_pool = stack.enter_context(tc.tile_pool(name="pack", bufs=3))
+        sum_pool = stack.enter_context(tc.tile_pool(name="sum", bufs=2))
+        z_pool = stack.enter_context(tc.tile_pool(name="z", bufs=2 * BATCH + 4))
+        w_pool = stack.enter_context(tc.tile_pool(name="w", bufs=2 * BATCH))
+        psum_rf = stack.enter_context(tc.psum_pool(name="psum_rf", bufs=2))
+        psum_bb = stack.enter_context(tc.psum_pool(name="psum_bb", bufs=2))
+        psum_acc = stack.enter_context(tc.psum_pool(name="psum_acc", bufs=4))
+        stack.enter_context(tc.manual_schedule())
+
+        bb_of = {}
+        rf_of = {}
+        total_of = {}
+        rf_t_of = {}
+        bb_t_of = {}
+        grouped_of = {}
+        codes_of = {}
+        scales_of = {}
+        acc_of = {}
+        z_of = {}
+        w_of = {}
+
+        def load(i):
+            bb = bb_pool.tile([P, QUADS, WIDTH], BF16)
+            if summed_by_adds(i):
+                nc.sync.dma_start(out=bb[:], in_=BB_feature[i * P : (i + 1) * P])
+            else:
+                nc.sync.dma_start(out=bb[:], in_=bb_rows[i])
+            bb_of[i] = bb
+            if i % QUADS == 0:
+                rf = rf_pool.tile([P, QUADS, WIDTH], BF16)
+                nc.sync.dma_start(out=rf[:], in_=rf_rows[i // QUADS])
+                rf_of[i // QUADS] = rf
+
+        bias = consts.tile([P, 2, WIDTH], BF16)
+        nc.scalar.dma_start(out=bias[:, 0, :], in_=b_rfrf.partition_broadcast(P))
+        nc.scalar.dma_start(out=bias[:, 1, :], in_=b_bbrf.partition_broadcast(P))
+
+        w_words = consts.tile([P, 2, 2 * WIDTH], U8, align_bytes=64)
+        w_planes = consts.tile([P, 2, WIDTH], U8, align_bytes=64)
+        nc.vector.memset(w_planes[:].rearrange("p o n -> p (o n)").bitcast(I32), 0)
+
+        load(0)
+        for o, (words, scales) in enumerate(
+            ((W_rfrf_words, W_rfrf_scales), (W_bbrf_words, W_bbrf_scales))
+        ):
+            nc.sync.dma_start(out=w_words[:, o, :].bitcast(I32), in_=words[0].bitcast(I32))
+            for q in range(4):
+                nc.sync.dma_start(
+                    out=w_planes[32 * q : 32 * q + 4, o, :].bitcast(I32),
+                    in_=scales[0, 4 * q : 4 * q + 4, :].bitcast(I32),
+                )
+        for i in range(1, LOAD_AHEAD):
+            load(i)
+
+        ident = consts.tile([P, P], F32)
+        make_identity(nc, ident[:])
+        ident_bf = consts.tile([P, P], BF16)
+        nc.vector.tensor_copy(out=ident_bf[:], in_=ident[:])
+        member_f32 = consts.tile([P, SAMPLES], F32)
+        nc.vector.tensor_reduce(
+            out=member_f32[:],
+            in_=ident[:].rearrange("p (j g) -> p j g", g=GROUPS),
+            axis=mybir.AxisListType.X,
+            op=ALU.add,
+        )
+        member = consts.tile([P, SAMPLES], BF16)
+        nc.vector.tensor_copy(out=member[:], in_=member_f32[:])
+
+        def add_nodes(i):
+            bb = bb_of[i]
+            pairs = sum_pool.tile([P, 2, WIDTH], F32)
+            nc.gpsimd.tensor_add(
+                out=pairs[:], in0=bb[:, 0:GROUPS:2, :], in1=bb[:, 1:GROUPS:2, :]
+            )
+            total = sum_pool.tile([P, WIDTH], BF16)
+            nc.gpsimd.tensor_add(out=total[:], in0=pairs[:, 0, :], in1=pairs[:, 1, :])
+            total_of[i] = total
+
+        def front(i):
+            rf_words = rf_of[i // QUADS][:, i % QUADS, :].bitcast(F32)
+            rf_t = psum_rf.tile([P, 2, P], F32)
+            for u in range(2):
+                nc.tensor.transpose(rf_t[:, u, :], rf_words[:, u : WIDTH // 2 : 2], ident[:])
+            rf_t_of[i] = rf_t
+            if summed_by_adds(i):
+                bb_t = psum_bb.tile([P, PACK, P], BF16, tag="bb_t")
+                for t in range(PACK):
+                    nc.tensor.transpose(bb_t[:, t, :], total_of[i][:, t:WIDTH:PACK], ident_bf[:])
+            else:
+                bb = bb_of[i]
+                bb_t = psum_bb.tile([P, PACK, P], F32, tag="bb_t")
+                for s in range(QUADS):
+                    for t in range(PACK):
+                        nc.tensor.matmul(
+                            out=bb_t[:, t, SAMPLES * s : SAMPLES * (s + 1)],
+                            lhsT=bb[:, s, t:WIDTH:PACK],
+                            rhs=member[:],
+                            start=True,
+                            stop=True,
+                        )
+            bb_t_of[i] = bb_t
+
+        def regroup(i):
+            grouped = pack_pool.tile([P, 2, P, PACK], BF16, align_bytes=64)
+            nc.vector.tensor_copy(
+                out=grouped[:, 0, :, :].bitcast(F32),
+                in_=rf_t_of[i][:].rearrange("p u r -> p r u"),
+            )
+            nc.vector.tensor_scalar_mul(
+                out=grouped[:, 1, :, :],
+                in0=bb_t_of[i][:].rearrange("p t r -> p r t"),
+                scalar1=1.0 / GROUPS,
+            )
+            grouped_of[i] = grouped
+
+        def quantise(i):
+            codes = pack_pool.tile([P, 2 * P], U32, align_bytes=64)
+            scales = pack_pool.tile([P, 2 * P], U8, align_bytes=64)
+            nc.vector.quantize_mx(
+                out=codes[:].bitcast(FP8X4),
+                scales=scales[:],
+                in_=grouped_of[i][:].rearrange("p o r t -> p (o r t)"),
+            )
+            codes_of[i] = codes
+            scales_of[i] = scales
+
+        def multiply(i):
+            for o in range(2):
+                acc = psum_acc.tile([P, WIDTH], F32)
+                nc.tensor.matmul_mx(
+                    out=acc[:],
+                    lhsT=codes_of[i][:, o * P : (o + 1) * P].bitcast(FP8X4),
+                    lhsT_scale=scales_of[i][:, o * P : (o + 1) * P],
+                    rhs=w_words[:, o, :].bitcast(FP4X4),
+                    rhs_scale=w_planes[:, o, :],
+                    start=True,
+                    stop=True,
+                )
+                acc_of[(i, o)] = acc
+
+        def add_bias(i):
+            z = z_pool.tile([P, 2, WIDTH], F32)
+            for o in range(2):
+                nc.vector.tensor_tensor(
+                    out=z[:, o, :], in0=acc_of[(i, o)][:], in1=bias[:, o, :], op=ALU.add
+                )
+            z_of[i] = z
+
+        def produce_step(i):
+            if i >= 0 and i + LOAD_AHEAD < TILES:
+                load(i + LOAD_AHEAD)
+            if 0 <= i + ADD_AHEAD < TILES and summed_by_adds(i + ADD_AHEAD):
+                add_nodes(i + ADD_AHEAD)
+            if 0 <= i + 2 < TILES:
+                front(i + 2)
+            if 0 <= i + 1 < TILES:
+                regroup(i + 1)
+            if 0 <= i < TILES:
+                add_bias(i)
+            if 0 <= i + 1 < TILES:
+                quantise(i + 1)
+                multiply(i + 1)
+
+        def sigmoid(i):
+            w = w_pool.tile([P, 2, WIDTH], F32)
+            nc.scalar.activation(out=w[:], in_=z_of[i][:], func=ACT.Sigmoid, scale=-1.0)
+            w_of[i] = w
+
+        def log(i):
+            nc.scalar.activation(out=w_of[i][:], in_=w_of[i][:], func=ACT.Ln, bias=TINY)
+
+        def tanh(i):
+            nc.scalar.activation(out=w_of[i][:], in_=w_of[i][:], func=ACT.Tanh, scale=-1.0)
+
+        def finish(i, last_batch):
+            w = w_of[i]
+            z = z_of[i]
+            if last_batch:
+                nc.vector.tensor_mul(out=w[:], in0=w[:], in1=z[:])
+            else:
+                nc.vector.tensor_mul(out=w[:, 0, :], in0=w[:, 0, :], in1=z[:, 0, :])
+                nc.gpsimd.tensor_mul(out=w[:, 1, :], in0=w[:, 1, :], in1=z[:, 1, :])
+            nc.gpsimd.tensor_add(out=w[:, 0, :], in0=w[:, 0, :], in1=w[:, 1, :])
+            nc.sync.dma_start(out=out[i * P : (i + 1) * P, :], in_=w[:, 0, :])
+
+        for i in range(-2, BATCH):
+            produce_step(i)
+        for k in range(BATCHES + 1):
+            for j in range(BATCH):
+                if k < BATCHES:
+                    sigmoid(k * BATCH + j)
+                if k > 0:
+                    tanh((k - 1) * BATCH + j)
+                    finish((k - 1) * BATCH + j, k == BATCHES)
+                if k + 1 < BATCHES:
+                    produce_step((k + 1) * BATCH + j)
+            if k < BATCHES:
+                for j in range(BATCH):
+                    log(k * BATCH + j)

@@ -61,7 +61,8 @@ def tile_gnn_layer_pa_t_kernel(
         w_pool = stack.enter_context(tc.tile_pool(name="w", bufs=2 * BATCH))
         psum_rf = stack.enter_context(tc.psum_pool(name="psum_rf", bufs=2))
         psum_bb = stack.enter_context(tc.psum_pool(name="psum_bb", bufs=2))
-        psum_acc = stack.enter_context(tc.psum_pool(name="psum_acc", bufs=4))
+        psum_acc = stack.enter_context(tc.psum_pool(name="psum_acc", bufs=3))
+        psum_idle = stack.enter_context(tc.psum_pool(name="psum_idle", bufs=1))
         stack.enter_context(tc.manual_schedule())
 
         bb_of = {}
@@ -123,6 +124,8 @@ def tile_gnn_layer_pa_t_kernel(
         member = consts.tile([P, SAMPLES], BF16)
         nc.vector.tensor_copy(out=member[:], in_=member_f32[:])
 
+        idle_bank = psum_idle.tile([P, WIDTH], F32)
+
         def add_nodes(i):
             bb = bb_of[i]
             pairs = sum_pool.tile([P, 2, WIDTH], F32)
@@ -133,29 +136,41 @@ def tile_gnn_layer_pa_t_kernel(
             nc.gpsimd.tensor_add(out=total[:], in0=pairs[:, 0, :], in1=pairs[:, 1, :])
             total_of[i] = total
 
-        def front(i):
+        def transpose_rf(i):
             rf_words = rf_of[i // QUADS][:, i % QUADS, :].bitcast(F32)
             rf_t = psum_rf.tile([P, 2, P], F32)
             for u in range(2):
                 nc.tensor.transpose(rf_t[:, u, :], rf_words[:, u : WIDTH // 2 : 2], ident[:])
             rf_t_of[i] = rf_t
+            bb_t_of[i] = psum_bb.tile(
+                [P, PACK, P], BF16 if summed_by_adds(i) else F32, name="bb_t", tag="bb_t"
+            )
+
+        def transpose_bb(i, s):
+            bb_t = bb_t_of[i]
             if summed_by_adds(i):
-                bb_t = psum_bb.tile([P, PACK, P], BF16, tag="bb_t")
-                for t in range(PACK):
-                    nc.tensor.transpose(bb_t[:, t, :], total_of[i][:, t:WIDTH:PACK], ident_bf[:])
+                nc.tensor.transpose(bb_t[:, s, :], total_of[i][:, s:WIDTH:PACK], ident_bf[:])
             else:
                 bb = bb_of[i]
-                bb_t = psum_bb.tile([P, PACK, P], F32, tag="bb_t")
-                for s in range(QUADS):
-                    for t in range(PACK):
-                        nc.tensor.matmul(
-                            out=bb_t[:, t, SAMPLES * s : SAMPLES * (s + 1)],
-                            lhsT=bb[:, s, t:WIDTH:PACK],
-                            rhs=member[:],
-                            start=True,
-                            stop=True,
-                        )
-            bb_t_of[i] = bb_t
+                for t in range(PACK):
+                    nc.tensor.matmul(
+                        out=bb_t[:, t, SAMPLES * s : SAMPLES * (s + 1)],
+                        lhsT=bb[:, s, t:WIDTH:PACK],
+                        rhs=member[:],
+                        start=True,
+                        stop=True,
+                    )
+
+        def keep_clock(i):
+            nc.tensor.matmul_mx(
+                out=idle_bank[:],
+                lhsT=codes_of[i][:, 0:P].bitcast(FP8X4),
+                lhsT_scale=scales_of[i][:, 0:P],
+                rhs=w_words[:, 0, :].bitcast(FP4X4),
+                rhs_scale=w_planes[:, 0, :],
+                start=True,
+                stop=True,
+            )
 
         def regroup(i):
             grouped = pack_pool.tile([P, 2, P, PACK], BF16, align_bytes=64)
@@ -181,19 +196,18 @@ def tile_gnn_layer_pa_t_kernel(
             codes_of[i] = codes
             scales_of[i] = scales
 
-        def multiply(i):
-            for o in range(2):
-                acc = psum_acc.tile([P, WIDTH], F32)
-                nc.tensor.matmul_mx(
-                    out=acc[:],
-                    lhsT=codes_of[i][:, o * P : (o + 1) * P].bitcast(FP8X4),
-                    lhsT_scale=scales_of[i][:, o * P : (o + 1) * P],
-                    rhs=w_words[:, o, :].bitcast(FP4X4),
-                    rhs_scale=w_planes[:, o, :],
-                    start=True,
-                    stop=True,
-                )
-                acc_of[(i, o)] = acc
+        def multiply(i, o):
+            acc = psum_acc.tile([P, WIDTH], F32)
+            nc.tensor.matmul_mx(
+                out=acc[:],
+                lhsT=codes_of[i][:, o * P : (o + 1) * P].bitcast(FP8X4),
+                lhsT_scale=scales_of[i][:, o * P : (o + 1) * P],
+                rhs=w_words[:, o, :].bitcast(FP4X4),
+                rhs_scale=w_planes[:, o, :],
+                start=True,
+                stop=True,
+            )
+            acc_of[(i, o)] = acc
 
         def add_bias(i):
             z = z_pool.tile([P, 2, WIDTH], F32)
@@ -208,15 +222,21 @@ def tile_gnn_layer_pa_t_kernel(
                 load(i + LOAD_AHEAD)
             if 0 <= i + ADD_AHEAD < TILES and summed_by_adds(i + ADD_AHEAD):
                 add_nodes(i + ADD_AHEAD)
-            if 0 <= i + 2 < TILES:
-                front(i + 2)
             if 0 <= i + 1 < TILES:
                 regroup(i + 1)
             if 0 <= i < TILES:
                 add_bias(i)
             if 0 <= i + 1 < TILES:
                 quantise(i + 1)
-                multiply(i + 1)
+            if 0 <= i + 2 < TILES:
+                transpose_rf(i + 2)
+            for s in range(QUADS):
+                if 0 <= i + 2 < TILES:
+                    transpose_bb(i + 2, s)
+                if s < 2 and 0 <= i and i + 2 < TILES:
+                    keep_clock(i)
+                if s >= 2 and 0 <= i + 1 < TILES:
+                    multiply(i + 1, s - 2)
 
         def sigmoid(i):
             w = w_pool.tile([P, 2, WIDTH], F32)

@@ -61,8 +61,7 @@ def tile_gnn_layer_pa_t_kernel(
         w_pool = stack.enter_context(tc.tile_pool(name="w", bufs=2 * BATCH))
         psum_rf = stack.enter_context(tc.psum_pool(name="psum_rf", bufs=2))
         psum_bb = stack.enter_context(tc.psum_pool(name="psum_bb", bufs=2))
-        psum_acc = stack.enter_context(tc.psum_pool(name="psum_acc", bufs=3))
-        psum_idle = stack.enter_context(tc.psum_pool(name="psum_idle", bufs=1))
+        psum_acc = stack.enter_context(tc.psum_pool(name="psum_acc", bufs=4))
         stack.enter_context(tc.manual_schedule())
 
         bb_of = {}
@@ -124,8 +123,6 @@ def tile_gnn_layer_pa_t_kernel(
         member = consts.tile([P, SAMPLES], BF16)
         nc.vector.tensor_copy(out=member[:], in_=member_f32[:])
 
-        idle_bank = psum_idle.tile([P, WIDTH], F32)
-
         def add_nodes(i):
             bb = bb_of[i]
             pairs = sum_pool.tile([P, 2, WIDTH], F32)
@@ -136,41 +133,29 @@ def tile_gnn_layer_pa_t_kernel(
             nc.gpsimd.tensor_add(out=total[:], in0=pairs[:, 0, :], in1=pairs[:, 1, :])
             total_of[i] = total
 
-        def transpose_rf(i):
+        def front(i):
             rf_words = rf_of[i // QUADS][:, i % QUADS, :].bitcast(F32)
             rf_t = psum_rf.tile([P, 2, P], F32)
             for u in range(2):
                 nc.tensor.transpose(rf_t[:, u, :], rf_words[:, u : WIDTH // 2 : 2], ident[:])
             rf_t_of[i] = rf_t
-            bb_t_of[i] = psum_bb.tile(
-                [P, PACK, P], BF16 if summed_by_adds(i) else F32, name="bb_t", tag="bb_t"
-            )
-
-        def transpose_bb(i, s):
-            bb_t = bb_t_of[i]
             if summed_by_adds(i):
-                nc.tensor.transpose(bb_t[:, s, :], total_of[i][:, s:WIDTH:PACK], ident_bf[:])
+                bb_t = psum_bb.tile([P, PACK, P], BF16, tag="bb_t")
+                for t in range(PACK):
+                    nc.tensor.transpose(bb_t[:, t, :], total_of[i][:, t:WIDTH:PACK], ident_bf[:])
             else:
                 bb = bb_of[i]
-                for t in range(PACK):
-                    nc.tensor.matmul(
-                        out=bb_t[:, t, SAMPLES * s : SAMPLES * (s + 1)],
-                        lhsT=bb[:, s, t:WIDTH:PACK],
-                        rhs=member[:],
-                        start=True,
-                        stop=True,
-                    )
-
-        def keep_clock(i):
-            nc.tensor.matmul_mx(
-                out=idle_bank[:],
-                lhsT=codes_of[i][:, 0:P].bitcast(FP8X4),
-                lhsT_scale=scales_of[i][:, 0:P],
-                rhs=w_words[:, 0, :].bitcast(FP4X4),
-                rhs_scale=w_planes[:, 0, :],
-                start=True,
-                stop=True,
-            )
+                bb_t = psum_bb.tile([P, PACK, P], F32, tag="bb_t")
+                for s in range(QUADS):
+                    for t in range(PACK):
+                        nc.tensor.matmul(
+                            out=bb_t[:, t, SAMPLES * s : SAMPLES * (s + 1)],
+                            lhsT=bb[:, s, t:WIDTH:PACK],
+                            rhs=member[:],
+                            start=True,
+                            stop=True,
+                        )
+            bb_t_of[i] = bb_t
 
         def regroup(i):
             grouped = pack_pool.tile([P, 2, P, PACK], BF16, align_bytes=64)
@@ -196,18 +181,19 @@ def tile_gnn_layer_pa_t_kernel(
             codes_of[i] = codes
             scales_of[i] = scales
 
-        def multiply(i, o):
-            acc = psum_acc.tile([P, WIDTH], F32)
-            nc.tensor.matmul_mx(
-                out=acc[:],
-                lhsT=codes_of[i][:, o * P : (o + 1) * P].bitcast(FP8X4),
-                lhsT_scale=scales_of[i][:, o * P : (o + 1) * P],
-                rhs=w_words[:, o, :].bitcast(FP4X4),
-                rhs_scale=w_planes[:, o, :],
-                start=True,
-                stop=True,
-            )
-            acc_of[(i, o)] = acc
+        def multiply(i):
+            for o in range(2):
+                acc = psum_acc.tile([P, WIDTH], F32)
+                nc.tensor.matmul_mx(
+                    out=acc[:],
+                    lhsT=codes_of[i][:, o * P : (o + 1) * P].bitcast(FP8X4),
+                    lhsT_scale=scales_of[i][:, o * P : (o + 1) * P],
+                    rhs=w_words[:, o, :].bitcast(FP4X4),
+                    rhs_scale=w_planes[:, o, :],
+                    start=True,
+                    stop=True,
+                )
+                acc_of[(i, o)] = acc
 
         def add_bias(i):
             z = z_pool.tile([P, 2, WIDTH], F32)
@@ -222,21 +208,15 @@ def tile_gnn_layer_pa_t_kernel(
                 load(i + LOAD_AHEAD)
             if 0 <= i + ADD_AHEAD < TILES and summed_by_adds(i + ADD_AHEAD):
                 add_nodes(i + ADD_AHEAD)
+            if 0 <= i + 2 < TILES:
+                front(i + 2)
             if 0 <= i + 1 < TILES:
                 regroup(i + 1)
             if 0 <= i < TILES:
                 add_bias(i)
             if 0 <= i + 1 < TILES:
                 quantise(i + 1)
-            if 0 <= i + 2 < TILES:
-                transpose_rf(i + 2)
-            for s in range(QUADS):
-                if 0 <= i + 2 < TILES:
-                    transpose_bb(i + 2, s)
-                if s < 2 and 0 <= i and i + 2 < TILES:
-                    keep_clock(i)
-                if s >= 2 and 0 <= i + 1 < TILES:
-                    multiply(i + 1, s - 2)
+                multiply(i + 1)
 
         def sigmoid(i):
             w = w_pool.tile([P, 2, WIDTH], F32)
@@ -249,14 +229,10 @@ def tile_gnn_layer_pa_t_kernel(
         def tanh(i):
             nc.scalar.activation(out=w_of[i][:], in_=w_of[i][:], func=ACT.Tanh, scale=-1.0)
 
-        def finish(i, last_batch):
+        def finish(i):
             w = w_of[i]
             z = z_of[i]
-            if last_batch:
-                nc.vector.tensor_mul(out=w[:], in0=w[:], in1=z[:])
-            else:
-                nc.vector.tensor_mul(out=w[:, 0, :], in0=w[:, 0, :], in1=z[:, 0, :])
-                nc.gpsimd.tensor_mul(out=w[:, 1, :], in0=w[:, 1, :], in1=z[:, 1, :])
+            nc.vector.tensor_mul(out=w[:], in0=w[:], in1=z[:])
             nc.gpsimd.tensor_add(out=w[:, 0, :], in0=w[:, 0, :], in1=w[:, 1, :])
             nc.sync.dma_start(out=out[i * P : (i + 1) * P, :], in_=w[:, 0, :])
 
@@ -268,7 +244,7 @@ def tile_gnn_layer_pa_t_kernel(
                     sigmoid(k * BATCH + j)
                 if k > 0:
                     tanh((k - 1) * BATCH + j)
-                    finish((k - 1) * BATCH + j, k == BATCHES)
+                    finish((k - 1) * BATCH + j)
                 if k + 1 < BATCHES:
                     produce_step((k + 1) * BATCH + j)
             if k < BATCHES:

@@ -229,11 +229,11 @@ def tile_gnn_layer_pa_t_kernel(
         def tanh(i):
             nc.scalar.activation(out=w_of[i][:], in_=w_of[i][:], func=ACT.Tanh, scale=-1.0)
 
-        def finish(i):
+        def finish(i, adder):
             w = w_of[i]
             z = z_of[i]
             nc.vector.tensor_mul(out=w[:], in0=w[:], in1=z[:])
-            nc.gpsimd.tensor_add(out=w[:, 0, :], in0=w[:, 0, :], in1=w[:, 1, :])
+            adder.tensor_add(out=w[:, 0, :], in0=w[:, 0, :], in1=w[:, 1, :])
             nc.sync.dma_start(out=out[i * P : (i + 1) * P, :], in_=w[:, 0, :])
 
         for i in range(-2, BATCH):
@@ -244,7 +244,7 @@ def tile_gnn_layer_pa_t_kernel(
                     sigmoid(k * BATCH + j)
                 if k > 0:
                     tanh((k - 1) * BATCH + j)
-                    finish((k - 1) * BATCH + j)
+                    finish((k - 1) * BATCH + j, nc.gpsimd if k + 1 < BATCHES else nc.vector)
                 if k + 1 < BATCHES:
                     produce_step((k + 1) * BATCH + j)
             if k < BATCHES:

@@ -21,8 +21,9 @@ WIDTH = 512
 TILES = TOKENS // P
 QUADS = 4
 SAMPLES = P // GROUPS
-BATCH = 8
-BATCHES = TILES // BATCH
+BATCHES = (4, 8, 8, 8, 4)
+BATCH = max(BATCHES)
+FIRST = tuple(sum(BATCHES[:k]) for k in range(len(BATCHES)))
 LOAD_AHEAD = 6
 ADD_AHEAD = 4
 TINY = 2.0 ** -60
@@ -236,17 +237,25 @@ def tile_gnn_layer_pa_t_kernel(
             adder.tensor_add(out=w[:, 0, :], in0=w[:, 0, :], in1=w[:, 1, :])
             nc.sync.dma_start(out=out[i * P : (i + 1) * P, :], in_=w[:, 0, :])
 
-        for i in range(-2, BATCH):
+        def tiles_of(k):
+            if 0 <= k < len(BATCHES):
+                return list(range(FIRST[k], FIRST[k] + BATCHES[k]))
+            return []
+
+        def share(tiles, j, steps):
+            return tiles[len(tiles) * j // steps : len(tiles) * (j + 1) // steps]
+
+        for i in range(-2, BATCHES[0]):
             produce_step(i)
-        for k in range(BATCHES + 1):
-            for j in range(BATCH):
-                if k < BATCHES:
-                    sigmoid(k * BATCH + j)
-                if k > 0:
-                    tanh((k - 1) * BATCH + j)
-                    finish((k - 1) * BATCH + j, nc.gpsimd if k + 1 < BATCHES else nc.vector)
-                if k + 1 < BATCHES:
-                    produce_step((k + 1) * BATCH + j)
-            if k < BATCHES:
-                for j in range(BATCH):
-                    log(k * BATCH + j)
+        for k in range(len(BATCHES) + 1):
+            steps = max(len(tiles_of(k)), len(tiles_of(k - 1)), len(tiles_of(k + 1)))
+            for j in range(steps):
+                for i in share(tiles_of(k), j, steps):
+                    sigmoid(i)
+                for i in share(tiles_of(k - 1), j, steps):
+                    tanh(i)
+                    finish(i, nc.gpsimd if tiles_of(k + 1) else nc.vector)
+                for i in share(tiles_of(k + 1), j, steps):
+                    produce_step(i)
+            for i in tiles_of(k):
+                log(i)

@@ -24,8 +24,9 @@ SAMPLES = P // GROUPS
 BATCHES = (4, 8, 8, 8, 4)
 BATCH = max(BATCHES)
 FIRST = tuple(sum(BATCHES[:k]) for k in range(len(BATCHES)))
-LOAD_AHEAD = 6
-ADD_AHEAD = 4
+LOAD_AHEAD = 8
+PIECES = 4
+ADD_AHEAD = 3
 TINY = 2.0 ** -60
 
 FLOPS = 2 * 2 * TOKENS * WIDTH * WIDTH
@@ -124,15 +125,16 @@ def tile_gnn_layer_pa_t_kernel(
         member = consts.tile([P, SAMPLES], BF16)
         nc.vector.tensor_copy(out=member[:], in_=member_f32[:])
 
-        def add_nodes(i):
+        def add_nodes(i, piece):
             bb = bb_of[i]
-            pairs = sum_pool.tile([P, 2, WIDTH], F32)
+            cols = slice(piece * WIDTH // PIECES, (piece + 1) * WIDTH // PIECES)
+            if piece == 0:
+                total_of[i] = sum_pool.tile([P, WIDTH], BF16, name="total")
+            pairs = sum_pool.tile([P, 2, WIDTH // PIECES], F32, name="pairs")
             nc.gpsimd.tensor_add(
-                out=pairs[:], in0=bb[:, 0:GROUPS:2, :], in1=bb[:, 1:GROUPS:2, :]
+                out=pairs[:], in0=bb[:, 0:GROUPS:2, cols], in1=bb[:, 1:GROUPS:2, cols]
             )
-            total = sum_pool.tile([P, WIDTH], BF16)
-            nc.gpsimd.tensor_add(out=total[:], in0=pairs[:, 0, :], in1=pairs[:, 1, :])
-            total_of[i] = total
+            nc.gpsimd.tensor_add(out=total_of[i][:, cols], in0=pairs[:, 0, :], in1=pairs[:, 1, :])
 
         def front(i):
             rf_words = rf_of[i // QUADS][:, i % QUADS, :].bitcast(F32)
@@ -207,8 +209,10 @@ def tile_gnn_layer_pa_t_kernel(
         def produce_step(i):
             if i >= 0 and i + LOAD_AHEAD < TILES:
                 load(i + LOAD_AHEAD)
-            if 0 <= i + ADD_AHEAD < TILES and summed_by_adds(i + ADD_AHEAD):
-                add_nodes(i + ADD_AHEAD)
+            for piece in range(PIECES):
+                summed = i + ADD_AHEAD + PIECES - 1 - piece
+                if 0 <= summed < TILES and summed_by_adds(summed):
+                    add_nodes(summed, piece)
             if 0 <= i + 2 < TILES:
                 front(i + 2)
             if 0 <= i + 1 < TILES:
@@ -245,7 +249,7 @@ def tile_gnn_layer_pa_t_kernel(
         def share(tiles, j, steps):
             return tiles[len(tiles) * j // steps : len(tiles) * (j + 1) // steps]
 
-        for i in range(-2, BATCHES[0]):
+        for i in range(-ADD_AHEAD, BATCHES[0]):
             produce_step(i)
         for k in range(len(BATCHES) + 1):
             steps = max(len(tiles_of(k)), len(tiles_of(k - 1)), len(tiles_of(k + 1)))

@@ -27,6 +27,7 @@ FIRST = tuple(sum(BATCHES[:k]) for k in range(len(BATCHES)))
 LOAD_AHEAD = 8
 PIECES = 4
 ADD_AHEAD = 3
+HELPED = BATCHES[0]
 TINY = 2.0 ** -60
 
 FLOPS = 2 * 2 * TOKENS * WIDTH * WIDTH
@@ -79,20 +80,29 @@ def tile_gnn_layer_pa_t_kernel(
         w_of = {}
 
         def load(i):
+            if i % QUADS == 0:
+                rf = rf_pool.tile([P, QUADS, WIDTH], BF16)
+                rf_of[i // QUADS] = rf
+                if i > 0:
+                    nc.sync.dma_start(out=rf[:], in_=rf_rows[i // QUADS])
             bb = bb_pool.tile([P, QUADS, WIDTH], BF16)
-            if summed_by_adds(i):
+            bb_of[i] = bb
+            if i == 0:
+                nc.sync.dma_start(out=rf[:, 0, :], in_=rf_rows[0][:, 0, :])
+                for half in (slice(0, QUADS // 2), slice(QUADS // 2, QUADS)):
+                    nc.sync.dma_start(out=bb[:, half, :], in_=bb_rows[0][:, half, :])
+            elif summed_by_adds(i):
                 nc.sync.dma_start(out=bb[:], in_=BB_feature[i * P : (i + 1) * P])
             else:
                 nc.sync.dma_start(out=bb[:], in_=bb_rows[i])
-            bb_of[i] = bb
-            if i % QUADS == 0:
-                rf = rf_pool.tile([P, QUADS, WIDTH], BF16)
-                nc.sync.dma_start(out=rf[:], in_=rf_rows[i // QUADS])
-                rf_of[i // QUADS] = rf
 
         bias = consts.tile([P, 2, WIDTH], BF16)
         nc.scalar.dma_start(out=bias[:, 0, :], in_=b_rfrf.partition_broadcast(P))
         nc.scalar.dma_start(out=bias[:, 1, :], in_=b_bbrf.partition_broadcast(P))
+
+        warm = consts.tile([P, 1], F32)
+        nc.vector.memset(warm[:], 0.0)
+        nc.scalar.activation(out=warm[:], in_=warm[:], func=ACT.Sigmoid)
 
         w_words = consts.tile([P, 2, 2 * WIDTH], U8, align_bytes=64)
         w_planes = consts.tile([P, 2, WIDTH], U8, align_bytes=64)
@@ -108,6 +118,7 @@ def tile_gnn_layer_pa_t_kernel(
                     out=w_planes[32 * q : 32 * q + 4, o, :].bitcast(I32),
                     in_=scales[0, 4 * q : 4 * q + 4, :].bitcast(I32),
                 )
+        nc.sync.dma_start(out=rf_of[0][:, 1:, :], in_=rf_rows[0][:, 1:, :])
         for i in range(1, LOAD_AHEAD):
             load(i)
 
@@ -162,15 +173,16 @@ def tile_gnn_layer_pa_t_kernel(
 
         def regroup(i):
             grouped = pack_pool.tile([P, 2, P, PACK], BF16, align_bytes=64)
-            nc.vector.tensor_copy(
-                out=grouped[:, 0, :, :].bitcast(F32),
-                in_=rf_t_of[i][:].rearrange("p u r -> p r u"),
-            )
-            nc.vector.tensor_scalar_mul(
-                out=grouped[:, 1, :, :],
-                in0=bb_t_of[i][:].rearrange("p t r -> p r t"),
-                scalar1=1.0 / GROUPS,
-            )
+            rf_out = grouped[:, 0, :, :].bitcast(F32)
+            rf_in = rf_t_of[i][:].rearrange("p u r -> p r u")
+            bb_out = grouped[:, 1, :, :]
+            bb_in = bb_t_of[i][:].rearrange("p t r -> p r t")
+            if i < HELPED:
+                nc.scalar.copy(out=rf_out, in_=rf_in)
+                nc.scalar.activation(out=bb_out, in_=bb_in, func=ACT.Copy, scale=1.0 / GROUPS)
+            else:
+                nc.vector.tensor_copy(out=rf_out, in_=rf_in)
+                nc.vector.tensor_scalar_mul(out=bb_out, in0=bb_in, scalar1=1.0 / GROUPS)
             grouped_of[i] = grouped
 
         def quantise(i):
@@ -247,15 +259,18 @@ def tile_gnn_layer_pa_t_kernel(
             return []
 
         def share(tiles, j, steps):
-            return tiles[len(tiles) * j // steps : len(tiles) * (j + 1) // steps]
+            return tiles[-(-len(tiles) * j // steps) : -(-len(tiles) * (j + 1) // steps)]
 
         for i in range(-ADD_AHEAD, BATCHES[0]):
             produce_step(i)
+            if i >= 0:
+                sigmoid(i)
         for k in range(len(BATCHES) + 1):
             steps = max(len(tiles_of(k)), len(tiles_of(k - 1)), len(tiles_of(k + 1)))
             for j in range(steps):
                 for i in share(tiles_of(k), j, steps):
-                    sigmoid(i)
+                    if k > 0:
+                        sigmoid(i)
                 for i in share(tiles_of(k - 1), j, steps):
                     tanh(i)
                     finish(i, nc.gpsimd if tiles_of(k + 1) else nc.vector)

@@ -27,7 +27,8 @@ FIRST = tuple(sum(BATCHES[:k]) for k in range(len(BATCHES)))
 LOAD_AHEAD = 8
 PIECES = 4
 ADD_AHEAD = 3
-HELPED = BATCHES[0]
+HELPED = 2
+LAG = 3
 TINY = 2.0 ** -60
 
 FLOPS = 2 * 2 * TOKENS * WIDTH * WIDTH
@@ -52,16 +53,16 @@ def tile_gnn_layer_pa_t_kernel(
     rf_rows = RF_feature.rearrange("(n s p) k -> n p s k", s=QUADS, p=P)
 
     def summed_by_adds(i):
-        return i % QUADS == QUADS - 1
+        return i % QUADS == QUADS - 1 and i >= BATCHES[0]
 
     with ExitStack() as stack:
         consts = stack.enter_context(tc.tile_pool(name="consts", bufs=1))
-        bb_pool = stack.enter_context(tc.tile_pool(name="bb", bufs=LOAD_AHEAD + 2))
+        bb_pool = stack.enter_context(tc.tile_pool(name="bb", bufs=LOAD_AHEAD + 1))
         rf_pool = stack.enter_context(tc.tile_pool(name="rf", bufs=3))
         pack_pool = stack.enter_context(tc.tile_pool(name="pack", bufs=3))
         sum_pool = stack.enter_context(tc.tile_pool(name="sum", bufs=2))
-        z_pool = stack.enter_context(tc.tile_pool(name="z", bufs=2 * BATCH + 4))
-        w_pool = stack.enter_context(tc.tile_pool(name="w", bufs=2 * BATCH))
+        z_pool = stack.enter_context(tc.tile_pool(name="z", bufs=2 * BATCH + 4 + LAG))
+        w_pool = stack.enter_context(tc.tile_pool(name="w", bufs=2 * BATCH + LAG))
         psum_rf = stack.enter_context(tc.psum_pool(name="psum_rf", bufs=2))
         psum_bb = stack.enter_context(tc.psum_pool(name="psum_bb", bufs=2))
         psum_acc = stack.enter_context(tc.psum_pool(name="psum_acc", bufs=4))
@@ -85,10 +86,11 @@ def tile_gnn_layer_pa_t_kernel(
                 rf_of[i // QUADS] = rf
                 if i > 0:
                     nc.sync.dma_start(out=rf[:], in_=rf_rows[i // QUADS])
+            if i < QUADS:
+                nc.sync.dma_start(out=rf_of[0][:, i, :], in_=rf_rows[0][:, i, :])
             bb = bb_pool.tile([P, QUADS, WIDTH], BF16)
             bb_of[i] = bb
             if i == 0:
-                nc.sync.dma_start(out=rf[:, 0, :], in_=rf_rows[0][:, 0, :])
                 for half in (slice(0, QUADS // 2), slice(QUADS // 2, QUADS)):
                     nc.sync.dma_start(out=bb[:, half, :], in_=bb_rows[0][:, half, :])
             elif summed_by_adds(i):
@@ -109,6 +111,7 @@ def tile_gnn_layer_pa_t_kernel(
         nc.vector.memset(w_planes[:].rearrange("p o n -> p (o n)").bitcast(I32), 0)
 
         load(0)
+        load(1)
         for o, (words, scales) in enumerate(
             ((W_rfrf_words, W_rfrf_scales), (W_bbrf_words, W_bbrf_scales))
         ):
@@ -118,8 +121,7 @@ def tile_gnn_layer_pa_t_kernel(
                     out=w_planes[32 * q : 32 * q + 4, o, :].bitcast(I32),
                     in_=scales[0, 4 * q : 4 * q + 4, :].bitcast(I32),
                 )
-        nc.sync.dma_start(out=rf_of[0][:, 1:, :], in_=rf_rows[0][:, 1:, :])
-        for i in range(1, LOAD_AHEAD):
+        for i in range(2, LOAD_AHEAD):
             load(i)
 
         ident = consts.tile([P, P], F32)
@@ -246,10 +248,11 @@ def tile_gnn_layer_pa_t_kernel(
         def tanh(i):
             nc.scalar.activation(out=w_of[i][:], in_=w_of[i][:], func=ACT.Tanh, scale=-1.0)
 
-        def finish(i, adder):
+        def product(i):
+            nc.vector.tensor_mul(out=w_of[i][:], in0=w_of[i][:], in1=z_of[i][:])
+
+        def total(i, adder):
             w = w_of[i]
-            z = z_of[i]
-            nc.vector.tensor_mul(out=w[:], in0=w[:], in1=z[:])
             adder.tensor_add(out=w[:, 0, :], in0=w[:, 0, :], in1=w[:, 1, :])
             nc.sync.dma_start(out=out[i * P : (i + 1) * P, :], in_=w[:, 0, :])
 
@@ -265,6 +268,8 @@ def tile_gnn_layer_pa_t_kernel(
             produce_step(i)
             if i >= 0:
                 sigmoid(i)
+        waiting = []
+        unsummed = []
         for k in range(len(BATCHES) + 1):
             steps = max(len(tiles_of(k)), len(tiles_of(k - 1)), len(tiles_of(k + 1)))
             for j in range(steps):
@@ -273,8 +278,18 @@ def tile_gnn_layer_pa_t_kernel(
                         sigmoid(i)
                 for i in share(tiles_of(k - 1), j, steps):
                     tanh(i)
-                    finish(i, nc.gpsimd if tiles_of(k + 1) else nc.vector)
+                    waiting.append(i)
+                while len(waiting) > (LAG if tiles_of(k + 1) else 0):
+                    i = waiting.pop(0)
+                    product(i)
+                    if tiles_of(k + 1):
+                        total(i, nc.gpsimd)
+                    else:
+                        unsummed.append(i)
+                        if len(unsummed) > 1:
+                            total(unsummed.pop(0), nc.vector)
                 for i in share(tiles_of(k + 1), j, steps):
                     produce_step(i)
             for i in tiles_of(k):
                 log(i)
+        total(unsummed.pop(0), nc.vector)

@@ -21,14 +21,14 @@ WIDTH = 512
 TILES = TOKENS // P
 QUADS = 4
 SAMPLES = P // GROUPS
-BATCHES = (4, 8, 8, 8, 4)
-BATCH = max(BATCHES)
+BATCHES = (3, 8, 9, 10, 2)
+NEIGHBOURS = max(a + b for a, b in zip(BATCHES, BATCHES[1:]))
 FIRST = tuple(sum(BATCHES[:k]) for k in range(len(BATCHES)))
 LOAD_AHEAD = 8
 PIECES = 4
 ADD_AHEAD = 3
-HELPED = 2
-LAG = 3
+HELPED = BATCHES[0]
+LAG = 0
 TINY = 2.0 ** -60
 
 FLOPS = 2 * 2 * TOKENS * WIDTH * WIDTH
@@ -53,7 +53,7 @@ def tile_gnn_layer_pa_t_kernel(
     rf_rows = RF_feature.rearrange("(n s p) k -> n p s k", s=QUADS, p=P)
 
     def summed_by_adds(i):
-        return i % QUADS == QUADS - 1 and i >= BATCHES[0]
+        return i % QUADS == QUADS - 1 and i > QUADS
 
     with ExitStack() as stack:
         consts = stack.enter_context(tc.tile_pool(name="consts", bufs=1))
@@ -61,8 +61,8 @@ def tile_gnn_layer_pa_t_kernel(
         rf_pool = stack.enter_context(tc.tile_pool(name="rf", bufs=3))
         pack_pool = stack.enter_context(tc.tile_pool(name="pack", bufs=3))
         sum_pool = stack.enter_context(tc.tile_pool(name="sum", bufs=2))
-        z_pool = stack.enter_context(tc.tile_pool(name="z", bufs=2 * BATCH + 4 + LAG))
-        w_pool = stack.enter_context(tc.tile_pool(name="w", bufs=2 * BATCH + LAG))
+        z_pool = stack.enter_context(tc.tile_pool(name="z", bufs=NEIGHBOURS + 4 + LAG))
+        w_pool = stack.enter_context(tc.tile_pool(name="w", bufs=NEIGHBOURS + LAG))
         psum_rf = stack.enter_context(tc.psum_pool(name="psum_rf", bufs=2))
         psum_bb = stack.enter_context(tc.psum_pool(name="psum_bb", bufs=2))
         psum_acc = stack.enter_context(tc.psum_pool(name="psum_acc", bufs=4))
@@ -220,20 +220,21 @@ def tile_gnn_layer_pa_t_kernel(
                 )
             z_of[i] = z
 
-        def produce_step(i):
-            if i >= 0 and i + LOAD_AHEAD < TILES:
-                load(i + LOAD_AHEAD)
-            for piece in range(PIECES):
-                summed = i + ADD_AHEAD + PIECES - 1 - piece
-                if 0 <= summed < TILES and summed_by_adds(summed):
-                    add_nodes(summed, piece)
-            if 0 <= i + 2 < TILES:
+        def produce_step(i, tiles):
+            if i in tiles:
+                if i + LOAD_AHEAD < TILES:
+                    load(i + LOAD_AHEAD)
+                for piece in range(PIECES):
+                    summed = i + ADD_AHEAD + PIECES - 1 - piece
+                    if summed < TILES and summed_by_adds(summed):
+                        add_nodes(summed, piece)
+            if i + 2 in tiles:
                 front(i + 2)
-            if 0 <= i + 1 < TILES:
+            if i + 1 in tiles:
                 regroup(i + 1)
-            if 0 <= i < TILES:
+            if i in tiles:
                 add_bias(i)
-            if 0 <= i + 1 < TILES:
+            if i + 1 in tiles:
                 quantise(i + 1)
                 multiply(i + 1)
 
@@ -264,10 +265,14 @@ def tile_gnn_layer_pa_t_kernel(
         def share(tiles, j, steps):
             return tiles[-(-len(tiles) * j // steps) : -(-len(tiles) * (j + 1) // steps)]
 
-        for i in range(-ADD_AHEAD, BATCHES[0]):
-            produce_step(i)
+        opening = range(0, BATCHES[0])
+        others = range(BATCHES[0], TILES)
+        for i in range(-2, BATCHES[0]):
+            produce_step(i, opening)
             if i >= 0:
                 sigmoid(i)
+        for i in range(BATCHES[0] - 2, BATCHES[0]):
+            produce_step(i, others)
         waiting = []
         unsummed = []
         for k in range(len(BATCHES) + 1):
@@ -289,7 +294,7 @@ def tile_gnn_layer_pa_t_kernel(
                         if len(unsummed) > 1:
                             total(unsummed.pop(0), nc.vector)
                 for i in share(tiles_of(k + 1), j, steps):
-                    produce_step(i)
+                    produce_step(i, others)
             for i in tiles_of(k):
                 log(i)
         total(unsummed.pop(0), nc.vector)

@@ -126,8 +126,6 @@ def tile_gnn_layer_pa_t_kernel(
 
         ident = consts.tile([P, P], F32)
         make_identity(nc, ident[:])
-        ident_bf = consts.tile([P, P], BF16)
-        nc.vector.tensor_copy(out=ident_bf[:], in_=ident[:])
         member_f32 = consts.tile([P, SAMPLES], F32)
         nc.vector.tensor_reduce(
             out=member_f32[:],
@@ -151,15 +149,19 @@ def tile_gnn_layer_pa_t_kernel(
 
         def front(i):
             rf_words = rf_of[i // QUADS][:, i % QUADS, :].bitcast(F32)
-            rf_t = psum_rf.tile([P, 2, P], F32)
-            for u in range(2):
-                nc.tensor.transpose(rf_t[:, u, :], rf_words[:, u : WIDTH // 2 : 2], ident[:])
-            rf_t_of[i] = rf_t
             if summed_by_adds(i):
-                bb_t = psum_bb.tile([P, PACK, P], BF16, tag="bb_t")
-                for t in range(PACK):
-                    nc.tensor.transpose(bb_t[:, t, :], total_of[i][:, t:WIDTH:PACK], ident_bf[:])
+                both_t = psum_bb.tile([P, 2, 2, P], F32, tag="bb_t")
+                for o, words in enumerate((rf_words, total_of[i][:].bitcast(F32))):
+                    for u in range(2):
+                        nc.tensor.transpose(
+                            both_t[:, o, u, :], words[:, u : WIDTH // 2 : 2], ident[:]
+                        )
+                bb_t_of[i] = both_t
             else:
+                rf_t = psum_rf.tile([P, 2, P], F32)
+                for u in range(2):
+                    nc.tensor.transpose(rf_t[:, u, :], rf_words[:, u : WIDTH // 2 : 2], ident[:])
+                rf_t_of[i] = rf_t
                 bb = bb_of[i]
                 bb_t = psum_bb.tile([P, PACK, P], F32, tag="bb_t")
                 for s in range(QUADS):
@@ -171,10 +173,16 @@ def tile_gnn_layer_pa_t_kernel(
                             start=True,
                             stop=True,
                         )
-            bb_t_of[i] = bb_t
+                bb_t_of[i] = bb_t
 
         def regroup(i):
             grouped = pack_pool.tile([P, 2, P, PACK], BF16, align_bytes=64)
+            grouped_of[i] = grouped
+            if summed_by_adds(i):
+                nc.vector.tensor_copy(
+                    out=grouped[:].bitcast(F32), in_=bb_t_of[i][:].rearrange("p o u r -> p o r u")
+                )
+                return
             rf_out = grouped[:, 0, :, :].bitcast(F32)
             rf_in = rf_t_of[i][:].rearrange("p u r -> p r u")
             bb_out = grouped[:, 1, :, :]
@@ -185,7 +193,6 @@ def tile_gnn_layer_pa_t_kernel(
             else:
                 nc.vector.tensor_copy(out=rf_out, in_=rf_in)
                 nc.vector.tensor_scalar_mul(out=bb_out, in0=bb_in, scalar1=1.0 / GROUPS)
-            grouped_of[i] = grouped
 
         def quantise(i):
             codes = pack_pool.tile([P, 2 * P], U32, align_bytes=64)
@@ -215,9 +222,19 @@ def tile_gnn_layer_pa_t_kernel(
         def add_bias(i):
             z = z_pool.tile([P, 2, WIDTH], F32)
             for o in range(2):
-                nc.vector.tensor_tensor(
-                    out=z[:, o, :], in0=acc_of[(i, o)][:], in1=bias[:, o, :], op=ALU.add
-                )
+                if o == 1 and summed_by_adds(i):
+                    nc.vector.scalar_tensor_tensor(
+                        out=z[:, o, :],
+                        in0=acc_of[(i, o)][:],
+                        scalar=1.0 / GROUPS,
+                        in1=bias[:, o, :],
+                        op0=ALU.mult,
+                        op1=ALU.add,
+                    )
+                else:
+                    nc.vector.tensor_tensor(
+                        out=z[:, o, :], in0=acc_of[(i, o)][:], in1=bias[:, o, :], op=ALU.add
+                    )
             z_of[i] = z
 
         def produce_step(i, tiles):

@@ -98,9 +98,12 @@ def tile_gnn_layer_pa_t_kernel(
             else:
                 nc.sync.dma_start(out=bb[:], in_=bb_rows[i])
 
-        bias = consts.tile([P, 2, WIDTH], BF16)
-        nc.scalar.dma_start(out=bias[:, 0, :], in_=b_rfrf.partition_broadcast(P))
-        nc.scalar.dma_start(out=bias[:, 1, :], in_=b_bbrf.partition_broadcast(P))
+        bias_rows = consts.tile([P, P], BF16)
+        nc.vector.memset(bias_rows[:], 0.0)
+        for o, b in enumerate((b_rfrf, b_bbrf)):
+            nc.scalar.dma_start(
+                out=bias_rows[4 * o : 4 * o + 4, :], in_=b.rearrange("(c p) -> c p", p=P)
+            )
 
         warm = consts.tile([P, 1], F32)
         nc.vector.memset(warm[:], 0.0)
@@ -126,6 +129,25 @@ def tile_gnn_layer_pa_t_kernel(
 
         ident = consts.tile([P, P], F32)
         make_identity(nc, ident[:])
+        ident_bf = consts.tile([P, P], BF16)
+        nc.vector.tensor_copy(out=ident_bf[:], in_=ident[:])
+        cols_t = psum_acc.tile([P, P], BF16, name="acc")
+        nc.tensor.transpose(cols_t[:], bias_rows[:], ident_bf[:])
+        bias_cols = consts.tile([P, 8], BF16)
+        nc.scalar.copy(out=bias_cols[:], in_=cols_t[:, 0:8])
+        bias = consts.tile([P, 2, WIDTH], BF16)
+
+        def spread_biases():
+            spread_t = psum_acc.tile([P, 8, P], BF16, name="acc")
+            for j in range(8):
+                nc.tensor.transpose(
+                    spread_t[:, j, :], bias_cols[:, j : j + 1].to_broadcast([P, P]), ident_bf[:]
+                )
+            nc.vector.tensor_copy(
+                out=bias[:].rearrange("p o n -> p (o n)"),
+                in_=spread_t[:].rearrange("p j n -> p (j n)"),
+            )
+
         member_f32 = consts.tile([P, SAMPLES], F32)
         nc.vector.tensor_reduce(
             out=member_f32[:],
@@ -286,6 +308,8 @@ def tile_gnn_layer_pa_t_kernel(
         others = range(BATCHES[0], TILES)
         for i in range(-2, BATCHES[0]):
             produce_step(i, opening)
+            if i == -2:
+                spread_biases()
             if i >= 0:
                 sigmoid(i)
         for i in range(BATCHES[0] - 2, BATCHES[0]):

@@ -131,21 +131,25 @@ def tile_gnn_layer_pa_t_kernel(
         make_identity(nc, ident[:])
         ident_bf = consts.tile([P, P], BF16)
         nc.vector.tensor_copy(out=ident_bf[:], in_=ident[:])
-        cols_t = psum_acc.tile([P, P], BF16, name="acc")
-        nc.tensor.transpose(cols_t[:], bias_rows[:], ident_bf[:])
         bias_cols = consts.tile([P, 8], BF16)
-        nc.scalar.copy(out=bias_cols[:], in_=cols_t[:, 0:8])
         bias = consts.tile([P, 2, WIDTH], BF16)
+        spread_of = {}
 
         def spread_biases():
+            cols_t = psum_acc.tile([P, P], BF16, name="acc")
+            nc.tensor.transpose(cols_t[:], bias_rows[:], ident_bf[:])
+            nc.scalar.copy(out=bias_cols[:], in_=cols_t[:, 0:8])
             spread_t = psum_acc.tile([P, 8, P], BF16, name="acc")
             for j in range(8):
                 nc.tensor.transpose(
                     spread_t[:, j, :], bias_cols[:, j : j + 1].to_broadcast([P, P]), ident_bf[:]
                 )
+            spread_of[0] = spread_t
+
+        def keep_biases():
             nc.vector.tensor_copy(
                 out=bias[:].rearrange("p o n -> p (o n)"),
-                in_=spread_t[:].rearrange("p j n -> p (j n)"),
+                in_=spread_of[0][:].rearrange("p j n -> p (j n)"),
             )
 
         member_f32 = consts.tile([P, SAMPLES], F32)
@@ -310,6 +314,8 @@ def tile_gnn_layer_pa_t_kernel(
             produce_step(i, opening)
             if i == -2:
                 spread_biases()
+            if i == -1:
+                keep_biases()
             if i >= 0:
                 sigmoid(i)
         for i in range(BATCHES[0] - 2, BATCHES[0]):

from contextlib import ExitStack

import concourse.mybir as mybir
from concourse.masks import make_identity

F32 = mybir.dt.float32
BF16 = mybir.dt.bfloat16
I32 = mybir.dt.int32
U32 = mybir.dt.uint32
U8 = mybir.dt.uint8
FP8X4 = mybir.dt.float8_e4m3fn_x4
FP4X4 = mybir.dt.float4_e2m1fn_x4
ACT = mybir.ActivationFunctionType
ALU = mybir.AluOpType

P = 128
PACK = 4
TOKENS = 4096
GROUPS = 4
WIDTH = 512
TILES = TOKENS // P
QUADS = 4
SAMPLES = P // GROUPS
BATCHES = (3, 8, 9, 10, 2)
NEIGHBOURS = max(a + b for a, b in zip(BATCHES, BATCHES[1:]))
FIRST = tuple(sum(BATCHES[:k]) for k in range(len(BATCHES)))
LOAD_AHEAD = 8
PIECES = 4
ADD_AHEAD = 3
HELPED = BATCHES[0]
LAG = 0
TINY = 2.0 ** -60

FLOPS = 2 * 2 * TOKENS * WIDTH * WIDTH


def tile_gnn_layer_pa_t_kernel(
    tc,
    BB_feature,
    RF_feature,
    W_rfrf_words,
    W_rfrf_scales,
    b_rfrf,
    W_bbrf_words,
    W_bbrf_scales,
    b_bbrf,
    out,
):
    nc = tc.nc
    bb_rows = BB_feature.rearrange("b g k -> (b g) k").rearrange(
        "(i s p) k -> i p s k", s=QUADS, p=P
    )
    rf_rows = RF_feature.rearrange("(n s p) k -> n p s k", s=QUADS, p=P)

    def summed_by_adds(i):
        return i % QUADS == QUADS - 1 and i > QUADS

    with ExitStack() as stack:
        consts = stack.enter_context(tc.tile_pool(name="consts", bufs=1))
        bb_pool = stack.enter_context(tc.tile_pool(name="bb", bufs=LOAD_AHEAD + 1))
        rf_pool = stack.enter_context(tc.tile_pool(name="rf", bufs=3))
        pack_pool = stack.enter_context(tc.tile_pool(name="pack", bufs=3))
        sum_pool = stack.enter_context(tc.tile_pool(name="sum", bufs=2))
        z_pool = stack.enter_context(tc.tile_pool(name="z", bufs=NEIGHBOURS + 4 + LAG))
        w_pool = stack.enter_context(tc.tile_pool(name="w", bufs=NEIGHBOURS + LAG))
        psum_rf = stack.enter_context(tc.psum_pool(name="psum_rf", bufs=2))
        psum_bb = stack.enter_context(tc.psum_pool(name="psum_bb", bufs=2))
        psum_acc = stack.enter_context(tc.psum_pool(name="psum_acc", bufs=4))
        stack.enter_context(tc.manual_schedule())

        bb_of = {}
        rf_of = {}
        total_of = {}
        rf_t_of = {}
        bb_t_of = {}
        grouped_of = {}
        codes_of = {}
        scales_of = {}
        acc_of = {}
        z_of = {}
        w_of = {}

        def load(i):
            if i % QUADS == 0:
                rf = rf_pool.tile([P, QUADS, WIDTH], BF16)
                rf_of[i // QUADS] = rf
                if i > 0:
                    nc.sync.dma_start(out=rf[:], in_=rf_rows[i // QUADS])
            if i < QUADS:
                nc.sync.dma_start(out=rf_of[0][:, i, :], in_=rf_rows[0][:, i, :])
            bb = bb_pool.tile([P, QUADS, WIDTH], BF16)
            bb_of[i] = bb
            if i == 0:
                for half in (slice(0, QUADS // 2), slice(QUADS // 2, QUADS)):
                    nc.sync.dma_start(out=bb[:, half, :], in_=bb_rows[0][:, half, :])
            elif summed_by_adds(i):
                nc.sync.dma_start(out=bb[:], in_=BB_feature[i * P : (i + 1) * P])
            else:
                nc.sync.dma_start(out=bb[:], in_=bb_rows[i])

        bias_rows = consts.tile([P, P], BF16)
        nc.vector.memset(bias_rows[:], 0.0)
        for o, b in enumerate((b_rfrf, b_bbrf)):
            nc.scalar.dma_start(
                out=bias_rows[4 * o : 4 * o + 4, :], in_=b.rearrange("(c p) -> c p", p=P)
            )

        warm = consts.tile([P, 1], F32)
        nc.vector.memset(warm[:], 0.0)
        nc.scalar.activation(out=warm[:], in_=warm[:], func=ACT.Sigmoid)

        w_words = consts.tile([P, 2, 2 * WIDTH], U8, align_bytes=64)
        w_planes = consts.tile([P, 2, WIDTH], U8, align_bytes=64)
        nc.vector.memset(w_planes[:].rearrange("p o n -> p (o n)").bitcast(I32), 0)

        load(0)
        load(1)
        for o, (words, scales) in enumerate(
            ((W_rfrf_words, W_rfrf_scales), (W_bbrf_words, W_bbrf_scales))
        ):
            nc.sync.dma_start(out=w_words[:, o, :].bitcast(I32), in_=words[0].bitcast(I32))
            for q in range(4):
                nc.sync.dma_start(
                    out=w_planes[32 * q : 32 * q + 4, o, :].bitcast(I32),
                    in_=scales[0, 4 * q : 4 * q + 4, :].bitcast(I32),
                )
        for i in range(2, LOAD_AHEAD):
            load(i)

        ident = consts.tile([P, P], F32)
        make_identity(nc, ident[:])
        ident_bf = consts.tile([P, P], BF16)
        nc.vector.tensor_copy(out=ident_bf[:], in_=ident[:])
        bias_cols = consts.tile([P, 8], BF16)
        bias = consts.tile([P, 2, WIDTH], BF16)
        spread_of = {}

        def spread_biases():
            cols_t = psum_acc.tile([P, P], BF16, name="acc")
            nc.tensor.transpose(cols_t[:], bias_rows[:], ident_bf[:])
            nc.scalar.copy(out=bias_cols[:], in_=cols_t[:, 0:8])
            spread_t = psum_acc.tile([P, 8, P], BF16, name="acc")
            for j in range(8):
                nc.tensor.transpose(
                    spread_t[:, j, :], bias_cols[:, j : j + 1].to_broadcast([P, P]), ident_bf[:]
                )
            spread_of[0] = spread_t

        def keep_biases():
            nc.vector.tensor_copy(
                out=bias[:].rearrange("p o n -> p (o n)"),
                in_=spread_of[0][:].rearrange("p j n -> p (j n)"),
            )

        member_f32 = consts.tile([P, SAMPLES], F32)
        nc.vector.tensor_reduce(
            out=member_f32[:],
            in_=ident[:].rearrange("p (j g) -> p j g", g=GROUPS),
            axis=mybir.AxisListType.X,
            op=ALU.add,
        )
        member = consts.tile([P, SAMPLES], BF16)
        nc.vector.tensor_copy(out=member[:], in_=member_f32[:])

        def add_nodes(i, piece):
            bb = bb_of[i]
            cols = slice(piece * WIDTH // PIECES, (piece + 1) * WIDTH // PIECES)
            if piece == 0:
                total_of[i] = sum_pool.tile([P, WIDTH], BF16, name="total")
            pairs = sum_pool.tile([P, 2, WIDTH // PIECES], F32, name="pairs")
            nc.gpsimd.tensor_add(
                out=pairs[:], in0=bb[:, 0:GROUPS:2, cols], in1=bb[:, 1:GROUPS:2, cols]
            )
            nc.gpsimd.tensor_add(out=total_of[i][:, cols], in0=pairs[:, 0, :], in1=pairs[:, 1, :])

        def front(i):
            rf_words = rf_of[i // QUADS][:, i % QUADS, :].bitcast(F32)
            if summed_by_adds(i):
                both_t = psum_bb.tile([P, 2, 2, P], F32, tag="bb_t")
                for o, words in enumerate((rf_words, total_of[i][:].bitcast(F32))):
                    for u in range(2):
                        nc.tensor.transpose(
                            both_t[:, o, u, :], words[:, u : WIDTH // 2 : 2], ident[:]
                        )
                bb_t_of[i] = both_t
            else:
                rf_t = psum_rf.tile([P, 2, P], F32)
                for u in range(2):
                    nc.tensor.transpose(rf_t[:, u, :], rf_words[:, u : WIDTH // 2 : 2], ident[:])
                rf_t_of[i] = rf_t
                bb = bb_of[i]
                bb_t = psum_bb.tile([P, PACK, P], F32, tag="bb_t")
                for s in range(QUADS):
                    for t in range(PACK):
                        nc.tensor.matmul(
                            out=bb_t[:, t, SAMPLES * s : SAMPLES * (s + 1)],
                            lhsT=bb[:, s, t:WIDTH:PACK],
                            rhs=member[:],
                            start=True,
                            stop=True,
                        )
                bb_t_of[i] = bb_t

        def regroup(i):
            grouped = pack_pool.tile([P, 2, P, PACK], BF16, align_bytes=64)
            grouped_of[i] = grouped
            if summed_by_adds(i):
                nc.vector.tensor_copy(
                    out=grouped[:].bitcast(F32), in_=bb_t_of[i][:].rearrange("p o u r -> p o r u")
                )
                return
            rf_out = grouped[:, 0, :, :].bitcast(F32)
            rf_in = rf_t_of[i][:].rearrange("p u r -> p r u")
            bb_out = grouped[:, 1, :, :]
            bb_in = bb_t_of[i][:].rearrange("p t r -> p r t")
            if i < HELPED:
                nc.scalar.copy(out=rf_out, in_=rf_in)
                nc.scalar.activation(out=bb_out, in_=bb_in, func=ACT.Copy, scale=1.0 / GROUPS)
            else:
                nc.vector.tensor_copy(out=rf_out, in_=rf_in)
                nc.vector.tensor_scalar_mul(out=bb_out, in0=bb_in, scalar1=1.0 / GROUPS)

        def quantise(i):
            codes = pack_pool.tile([P, 2 * P], U32, align_bytes=64)
            scales = pack_pool.tile([P, 2 * P], U8, align_bytes=64)
            nc.vector.quantize_mx(
                out=codes[:].bitcast(FP8X4),
                scales=scales[:],
                in_=grouped_of[i][:].rearrange("p o r t -> p (o r t)"),
            )
            codes_of[i] = codes
            scales_of[i] = scales

        def multiply(i):
            for o in range(2):
                acc = psum_acc.tile([P, WIDTH], F32)
                nc.tensor.matmul_mx(
                    out=acc[:],
                    lhsT=codes_of[i][:, o * P : (o + 1) * P].bitcast(FP8X4),
                    lhsT_scale=scales_of[i][:, o * P : (o + 1) * P],
                    rhs=w_words[:, o, :].bitcast(FP4X4),
                    rhs_scale=w_planes[:, o, :],
                    start=True,
                    stop=True,
                )
                acc_of[(i, o)] = acc

        def add_bias(i):
            z = z_pool.tile([P, 2, WIDTH], F32)
            for o in range(2):
                if o == 1 and summed_by_adds(i):
                    nc.vector.scalar_tensor_tensor(
                        out=z[:, o, :],
                        in0=acc_of[(i, o)][:],
                        scalar=1.0 / GROUPS,
                        in1=bias[:, o, :],
                        op0=ALU.mult,
                        op1=ALU.add,
                    )
                else:
                    nc.vector.tensor_tensor(
                        out=z[:, o, :], in0=acc_of[(i, o)][:], in1=bias[:, o, :], op=ALU.add
                    )
            z_of[i] = z

        def produce_step(i, tiles):
            if i in tiles:
                if i + LOAD_AHEAD < TILES:
                    load(i + LOAD_AHEAD)
                for piece in range(PIECES):
                    summed = i + ADD_AHEAD + PIECES - 1 - piece
                    if summed < TILES and summed_by_adds(summed):
                        add_nodes(summed, piece)
            if i + 2 in tiles:
                front(i + 2)
            if i + 1 in tiles:
                regroup(i + 1)
            if i in tiles:
                add_bias(i)
            if i + 1 in tiles:
                quantise(i + 1)
                multiply(i + 1)

        def sigmoid(i):
            w = w_pool.tile([P, 2, WIDTH], F32)
            nc.scalar.activation(out=w[:], in_=z_of[i][:], func=ACT.Sigmoid, scale=-1.0)
            w_of[i] = w

        def log(i):
            nc.scalar.activation(out=w_of[i][:], in_=w_of[i][:], func=ACT.Ln, bias=TINY)

        def tanh(i):
            nc.scalar.activation(out=w_of[i][:], in_=w_of[i][:], func=ACT.Tanh, scale=-1.0)

        def product(i):
            nc.vector.tensor_mul(out=w_of[i][:], in0=w_of[i][:], in1=z_of[i][:])

        def total(i, adder):
            w = w_of[i]
            adder.tensor_add(out=w[:, 0, :], in0=w[:, 0, :], in1=w[:, 1, :])
            nc.sync.dma_start(out=out[i * P : (i + 1) * P, :], in_=w[:, 0, :])

        def tiles_of(k):
            if 0 <= k < len(BATCHES):
                return list(range(FIRST[k], FIRST[k] + BATCHES[k]))
            return []

        def share(tiles, j, steps):
            return tiles[-(-len(tiles) * j // steps) : -(-len(tiles) * (j + 1) // steps)]

        opening = range(0, BATCHES[0])
        others = range(BATCHES[0], TILES)
        for i in range(-2, BATCHES[0]):
            produce_step(i, opening)
            if i == -2:
                spread_biases()
            if i == -1:
                keep_biases()
            if i >= 0:
                sigmoid(i)
        for i in range(BATCHES[0] - 2, BATCHES[0]):
            produce_step(i, others)
        waiting = []
        unsummed = []
        for k in range(len(BATCHES) + 1):
            steps = max(len(tiles_of(k)), len(tiles_of(k - 1)), len(tiles_of(k + 1)))
            for j in range(steps):
                for i in share(tiles_of(k), j, steps):
                    if k > 0:
                        sigmoid(i)
                for i in share(tiles_of(k - 1), j, steps):
                    tanh(i)
                    waiting.append(i)
                while len(waiting) > (LAG if tiles_of(k + 1) else 0):
                    i = waiting.pop(0)
                    product(i)
                    if tiles_of(k + 1):
                        total(i, nc.gpsimd)
                    else:
                        unsummed.append(i)
                        if len(unsummed) > 1:
                            total(unsummed.pop(0), nc.vector)
                for i in share(tiles_of(k + 1), j, steps):
                    produce_step(i, others)
            for i in tiles_of(k):
                log(i)
        total(unsummed.pop(0), nc.vector)
